import numpy as np
import ml_dtypes


def mxq(x, axis, fmt="e4m3"):
    dtype, down = {"e4m3": (ml_dtypes.float8_e4m3fn, 7), "e5m2": (ml_dtypes.float8_e5m2, 14)}[fmt]
    v = np.moveaxis(np.asarray(x, np.float32).astype(ml_dtypes.bfloat16).astype(np.float64), axis, -1)
    blocks = v.reshape(v.shape[:-1] + (-1, 32))
    amax = np.abs(blocks).max(-1, keepdims=True)
    byte = np.maximum(np.where(amax > 0, np.frexp(amax)[1] - 1 + 127, 0) - down, 1)
    scale = np.exp2(byte - 127.0)
    codes = (blocks / scale).astype(np.float32).astype(dtype).astype(np.float64)
    return np.moveaxis((codes * scale).reshape(v.shape), -1, axis)


WIDE = False


def mx_kscale(k):
    if not WIDE:
        return np.ones(k)
    levels = np.array([10, -10, 5, -5, 0])
    a = np.random.permutation(np.resize(levels, k // 512 * 4)).reshape(k // 512, 4)
    idx = np.arange(k)
    return np.exp2(a[idx // 512, idx % 128 // 32])


BF16 = ml_dtypes.bfloat16


def bf(x):
    return np.asarray(x, np.float32).astype(BF16)


def f64(x):
    return np.asarray(x).astype(np.float64)


B, H, K = 128, 512, 512
R = H ** -0.25


def setup_inputs():
    s = mx_kscale(H)
    return {
        "encoder_final_state": bf(np.random.standard_normal((B, H)) * s),
        "W_mu": bf(np.random.standard_normal((H, H)) * 0.55 * R / np.sqrt(H) / s[None, :]),
        "b_mu": bf(np.random.standard_normal(H) * 0.3 * R),
        "W_ls": bf(np.random.standard_normal((H, H)) * 0.5 / np.sqrt(H) / s[None, :]),
        "b_ls": bf(np.random.standard_normal(H) * 0.1),
        "mu_c": bf(np.random.standard_normal((K, H)) * 0.5 * R),
        "log_sigma_sq_c": bf(np.random.standard_normal((K, H)) * 0.4),
        "eps_z": bf(np.random.standard_normal((B, H)) * 0.55 * R),
    }


def reference(encoder_final_state, W_mu, b_mu, W_ls, b_ls, mu_c, log_sigma_sq_c, eps_z):
    xq = mxq(f64(encoder_final_state), 1, "e4m3")
    mu_z = (xq @ mxq(f64(W_mu), 1, "e4m3").T) + f64(b_mu)
    ls_z = (xq @ mxq(f64(W_ls), 1, "e4m3").T) + f64(b_ls)
    z = mu_z + np.exp(0.5 * ls_z) * f64(eps_z)
    inv_sig = np.exp(-f64(log_sigma_sq_c))
    mu_inv = f64(mu_c) * inv_sig
    c2 = np.sum(f64(mu_c) * mu_inv, axis=-1)
    d = (mxq(z * z, 1, "e4m3") @ mxq(inv_sig, 1, "e4m3").T) - 2.0 * (mxq(z, 1, "e4m3") @ mxq(mu_inv, 1, "e4m3").T) + c2[None, :]
    g = -d
    e = np.exp(g - g.max(-1, keepdims=True))
    att = e / e.sum(-1, keepdims=True)
    return z, att

@@ -1,0 +1,300 @@
+from contextlib import ExitStack
+
+import concourse.mybir as mybir
+from concourse.masks import make_identity
+
+F32 = mybir.dt.float32
+BF16 = mybir.dt.bfloat16
+U32 = mybir.dt.uint32
+U8 = mybir.dt.uint8
+FP8X4 = mybir.dt.float8_e4m3fn_x4
+ACT = mybir.ActivationFunctionType
+ALU = mybir.AluOpType
+AX = mybir.AxisListType
+
+P = 128
+PACK = 4
+B = 128
+H = 512
+C = 512
+HALF = 256
+
+FLOPS = 4 * 2 * B * H * 512
+
+
+def tile_latent_pa_s_kernel(
+    tc, encoder_final_state, W_mu, b_mu, W_ls, b_ls, mu_c, log_sigma_sq_c, eps_z, out_0, out_1
+):
+    nc = tc.nc
+    with ExitStack() as ctx:
+        keep = ctx.enter_context(tc.tile_pool(name="keep", bufs=1))
+        psum = ctx.enter_context(tc.psum_pool(name="psum", bufs=2))
+        ctx.enter_context(tc.manual_schedule())
+
+        ident = keep.tile([P, P], F32)
+        make_identity(nc, ident[:])
+
+        bias_rows = keep.tile([P, P], BF16)
+        nc.vector.memset(bias_rows[:], 0.0)
+        ident_bf = keep.tile([P, P], BF16)
+        nc.vector.tensor_copy(out=ident_bf[:], in_=ident[:])
+        nc.scalar.dma_start(out=bias_rows[0:PACK, :], in_=b_ls.rearrange("(t p) -> t p", p=P))
+        nc.scalar.dma_start(out=bias_rows[PACK : 2 * PACK, :], in_=b_mu.rearrange("(t p) -> t p", p=P))
+        lsc_rows = keep.tile([P, PACK, H], BF16)
+        muc_rows = keep.tile([P, PACK, H], BF16)
+        lsc_dram = log_sigma_sq_c.rearrange("(q r) h -> q r h", r=PACK)
+        muc_dram = mu_c.rearrange("(q r) h -> q r h", r=PACK)
+        for g in range(2):
+            nc.sync.dma_start(out=lsc_rows[:, 2 * g : 2 * g + 2, :], in_=lsc_dram[:, 2 * g : 2 * g + 2, :])
+            nc.sync.dma_start(out=muc_rows[:, 2 * g : 2 * g + 2, :], in_=muc_dram[:, 2 * g : 2 * g + 2, :])
+        x_rows = keep.tile([P, H], BF16)
+        nc.sync.dma_start(out=x_rows[:], in_=encoder_final_state)
+        w_rows = {}
+        for name, w_dram in (("ls", W_ls), ("mu", W_mu)):
+            w_rows[name] = keep.tile([P, PACK, H], BF16, name="w_rows_" + name)
+            nc.sync.dma_start(out=w_rows[name][:], in_=w_dram.rearrange("(t q) k -> q t k", q=P))
+        eps_rows = keep.tile([P, H], BF16)
+        nc.sync.dma_start(out=eps_rows[:], in_=eps_z)
+
+        inv_nat = keep.tile([P, PACK, H], F32)
+        minv_nat = keep.tile([P, PACK, H], F32)
+        prod = keep.tile([P, PACK, H], F32)
+        c2_col = keep.tile([P, PACK], F32)
+        natural = {"inv": inv_nat, "minv": minv_nat}
+        grouped = {}
+        codes = {}
+        scales = {}
+        for name in ("inv", "minv", "ls", "mu"):
+            grouped[name] = keep.tile([P, C, PACK], BF16, align_bytes=64, name="grouped_" + name)
+            codes[name] = keep.tile([P, C], U32, align_bytes=64, name="codes_" + name)
+            scales[name] = keep.tile([P, C], U8, align_bytes=64, name="scales_" + name)
+        banks = {}
+
+        def quantise_half(name, g):
+            cols = slice(g * HALF, (g + 1) * HALF)
+            nc.vector.quantize_mx(
+                out=codes[name][:, cols].bitcast(FP8X4),
+                scales=scales[name][:, cols],
+                in_=grouped[name][:, cols, :].rearrange("p n t -> p (n t)"),
+            )
+
+        def cluster_products(r):
+            nc.scalar.activation(out=inv_nat[:, r, :], in_=lsc_rows[:, r, :], func=ACT.Exp, scale=-1.0)
+            nc.vector.tensor_tensor(
+                out=minv_nat[:, r, :], in0=muc_rows[:, r, :], in1=inv_nat[:, r, :], op=ALU.mult
+            )
+
+        def cluster_c2(r):
+            nc.vector.scalar_tensor_tensor(
+                out=prod[:, r, :],
+                in0=minv_nat[:, r, :],
+                scalar=1.0,
+                in1=muc_rows[:, r, :],
+                op0=ALU.mult,
+                op1=ALU.mult,
+                accum_out=c2_col[:, r : r + 1],
+            )
+
+        def cluster_transpose(name, r):
+            bank = psum.tile([P, PACK, P], F32, tag="ct", bufs=3, name="cluster_bank")
+            for t in range(PACK):
+                nc.tensor.transpose(bank[:, t, :], natural[name][:, r, t * P : (t + 1) * P], ident[:])
+            banks[name, r] = bank
+
+        def cluster_round(copy, name, r):
+            copy(
+                out=grouped[name][:, r * P : (r + 1) * P, :],
+                in_=banks[name, r][:].rearrange("p t q -> p q t"),
+            )
+
+        def word_transposes(bank_cols, rows):
+            words = rows.bitcast(F32)
+            for u in range(2):
+                nc.tensor.transpose(bank_cols[:, u, :], words[:, u * P : (u + 1) * P], ident[:])
+
+        def weight_transpose(name, g):
+            bank = psum.tile([P, 2, HALF], F32, tag="wt", name="weight_bank")
+            for i in range(2):
+                word_transposes(bank[:, :, i * P : (i + 1) * P], w_rows[name][:, 2 * g + i, :])
+            banks[name, g] = bank
+
+        def weight_regroup(name, g):
+            nc.scalar.copy(
+                out=grouped[name][:, g * HALF : (g + 1) * HALF, :].bitcast(F32),
+                in_=banks[name, g][:].rearrange("p u n -> p n u"),
+            )
+
+        def first_product(name):
+            acc = psum.tile([P, PACK, B], F32, tag="s1", name="s1_" + name)
+            for t in range(PACK):
+                nc.tensor.matmul_mx(
+                    out=acc[:, t, :],
+                    lhsT=codes[name][:, t * P : (t + 1) * P].bitcast(FP8X4),
+                    lhsT_scale=scales[name][:, t * P : (t + 1) * P],
+                    rhs=x_codes[:].bitcast(FP8X4),
+                    rhs_scale=x_scales[:],
+                    start=True,
+                    stop=True,
+                )
+            return acc
+
+        for r in range(PACK):
+            cluster_products(r)
+        cluster_transpose("inv", 0)
+        cluster_transpose("inv", 1)
+        cluster_transpose("minv", 0)
+
+        x_bank = psum.tile([P, 2, B], F32, tag="xe", bufs=1)
+        word_transposes(x_bank[:], x_rows[:])
+        x_grouped = keep.tile([P, B, PACK], BF16, align_bytes=64)
+        nc.vector.tensor_copy(out=x_grouped[:].bitcast(F32), in_=x_bank[:].rearrange("p u n -> p n u"))
+        x_codes = keep.tile([P, B], U32, align_bytes=64)
+        x_scales = keep.tile([P, B], U8, align_bytes=64)
+        nc.vector.quantize_mx(
+            out=x_codes[:].bitcast(FP8X4),
+            scales=x_scales[:],
+            in_=x_grouped[:].rearrange("p n t -> p (n t)"),
+        )
+
+        cluster_round(nc.scalar.copy, "inv", 0)
+        cluster_round(nc.scalar.copy, "inv", 1)
+        cluster_round(nc.scalar.copy, "minv", 0)
+        cluster_c2(0)
+        cluster_c2(1)
+
+        weight_transpose("ls", 0)
+        weight_transpose("ls", 1)
+        cluster_transpose("minv", 1)
+        weight_regroup("ls", 0)
+        weight_regroup("ls", 1)
+        cluster_round(nc.vector.tensor_copy, "minv", 1)
+        quantise_half("ls", 0)
+        quantise_half("ls", 1)
+        cluster_c2(2)
+        weight_transpose("mu", 0)
+        weight_transpose("mu", 1)
+        weight_regroup("mu", 0)
+        weight_regroup("mu", 1)
+        quantise_half("mu", 0)
+        quantise_half("mu", 1)
+
+        eb_bank = psum.tile([P, PACK + 1, P], BF16, tag="xe", bufs=1)
+        for t in range(PACK):
+            nc.tensor.transpose(eb_bank[:, t, :], eps_rows[:, t * P : (t + 1) * P], ident_bf[:])
+        nc.tensor.transpose(eb_bank[:, PACK, :], bias_rows[:], ident_bf[:])
+        half_bls = keep.tile([P, PACK], F32)
+        bmu = keep.tile([P, PACK], F32)
+        nc.vector.tensor_scalar_mul(out=half_bls[:], in0=eb_bank[:, PACK, 0:PACK], scalar1=0.5)
+        nc.vector.tensor_copy(out=bmu[:], in_=eb_bank[:, PACK, PACK : 2 * PACK])
+
+        cluster_transpose("inv", 2)
+        cluster_transpose("inv", 3)
+        ls_acc = first_product("ls")
+        cluster_round(nc.scalar.copy, "inv", 2)
+        cluster_transpose("minv", 2)
+        mu_acc = first_product("mu")
+        cluster_transpose("minv", 3)
+        cluster_c2(3)
+
+        c2_bank = psum.tile([P, C], F32, tag="wt")
+        for r in range(PACK):
+            nc.tensor.matmul(
+                out=c2_bank[:, r * P : (r + 1) * P],
+                lhsT=c2_col[:, r : r + 1].to_broadcast([P, P]),
+                rhs=ident[:],
+                start=True,
+                stop=True,
+            )
+        quantise_half("inv", 0)
+        quantise_half("minv", 0)
+
+        s_sb = keep.tile([P, PACK, B], F32)
+        w_sb = keep.tile([P, PACK, B], F32)
+        z_sb = keep.tile([P, PACK, B], F32)
+        z_bank = psum.tile([P, PACK, P], F32, tag="wt")
+        for t in range(PACK):
+            nc.scalar.activation(
+                out=s_sb[:, t, :], in_=ls_acc[:, t, :], func=ACT.Exp, bias=half_bls[:, t : t + 1], scale=0.5
+            )
+
+        def scaled_noise(t):
+            nc.vector.tensor_tensor(out=w_sb[:, t, :], in0=s_sb[:, t, :], in1=eb_bank[:, t, :], op=ALU.mult)
+
+        def latent(t):
+            nc.vector.scalar_tensor_tensor(
+                out=z_sb[:, t, :],
+                in0=mu_acc[:, t, :],
+                scalar=bmu[:, t : t + 1],
+                in1=w_sb[:, t, :],
+                op0=ALU.add,
+                op1=ALU.add,
+            )
+            nc.tensor.transpose(z_bank[:, t, :], z_sb[:, t, :], ident[:])
+
+        scaled_noise(0)
+        for t in range(1, PACK):
+            scaled_noise(t)
+            latent(t - 1)
+        latent(PACK - 1)
+
+        cluster_round(nc.scalar.copy, "inv", 3)
+        cluster_round(nc.scalar.copy, "minv", 2)
+        cluster_round(nc.scalar.copy, "minv", 3)
+        quantise_half("inv", 1)
+
+        z_grouped = keep.tile([P, 2, B, PACK], BF16, align_bytes=64)
+        z_view = z_sb[:].rearrange("p t b -> p b t")
+        nc.vector.tensor_scalar_mul(out=z_grouped[:, 0, :, :], in0=z_view, scalar1=-2.0)
+        nc.scalar.activation(out=z_grouped[:, 1, :, :], in_=z_view, func=ACT.Square)
+        quantise_half("minv", 1)
+        z_codes = keep.tile([P, 2 * B], U32, align_bytes=64)
+        z_scales = keep.tile([P, 2 * B], U8, align_bytes=64)
+        nc.vector.quantize_mx(
+            out=z_codes[:].bitcast(FP8X4),
+            scales=z_scales[:],
+            in_=z_grouped[:].rearrange("p a b t -> p (a b t)"),
+        )
+        c2_sb = keep.tile([P, C], F32)
+        nc.scalar.copy(out=c2_sb[:], in_=c2_bank[:])
+
+        z_out = keep.tile([P, H], F32)
+        nc.scalar.copy(out=z_out[:], in_=z_bank[:].rearrange("b t p -> b (t p)"))
+        nc.sync.dma_start(out=out_0, in_=z_out[:])
+
+        d_bank = psum.tile([P, C], F32, tag="ct", bufs=3)
+        nc.tensor.matmul_mx(
+            out=d_bank[:],
+            lhsT=z_codes[:, B : 2 * B].bitcast(FP8X4),
+            lhsT_scale=z_scales[:, B : 2 * B],
+            rhs=codes["inv"][:].bitcast(FP8X4),
+            rhs_scale=scales["inv"][:],
+            start=True,
+            stop=False,
+        )
+        nc.tensor.matmul_mx(
+            out=d_bank[:],
+            lhsT=z_codes[:, 0:B].bitcast(FP8X4),
+            lhsT_scale=z_scales[:, 0:B],
+            rhs=codes["minv"][:].bitcast(FP8X4),
+            rhs_scale=scales["minv"][:],
+            start=False,
+            stop=True,
+        )
+        d_sb = keep.tile([P, C], F32)
+        nc.vector.tensor_tensor(out=d_sb[:], in0=d_bank[:], in1=c2_sb[:], op=ALU.add)
+
+        d_min = keep.tile([P, 1], F32)
+        nc.vector.tensor_reduce(out=d_min[:], in_=d_sb[:], axis=AX.X, op=ALU.min)
+        e_sb = keep.tile([P, C], F32)
+        e_sum = keep.tile([P, 1], F32)
+        nc.scalar.activation(
+            out=e_sb[:], in_=d_sb[:], func=ACT.Exp, bias=d_min[:], scale=-1.0, accum_out=e_sum[:]
+        )
+        e_rec = keep.tile([P, 1], F32)
+        nc.vector.reciprocal(out=e_rec[:], in_=e_sum[:])
+        att = keep.tile([P, P, PACK], F32)
+        e_view = e_sb[:].rearrange("b (r q) -> b q r", r=PACK)
+        nc.vector.tensor_scalar_mul(out=att[:, 0:64, :], in0=e_view[:, 0:64, :], scalar1=e_rec[:])
+        nc.scalar.activation(out=att[:, 64:P, :], in_=e_view[:, 64:P, :], func=ACT.Copy, scale=e_rec[:])
+        nc.sync.dma_start(out=out_1[:, 0:HALF], in_=att[:, 0:64, :].rearrange("b q r -> b (q r)"))
+        nc.scalar.dma_start(out=out_1[:, HALF:C], in_=att[:, 64:P, :].rearrange("b q r -> b (q r)"))

@@ -34,33 +34,42 @@ def tile_latent_pa_s_kernel(
         ident = keep.tile([P, P], F32)
         make_identity(nc, ident[:])
 
-        bias_rows = keep.tile([P, P], BF16)
+        bias_rows = keep.tile([P, H], BF16)
         nc.vector.memset(bias_rows[:], 0.0)
-        ident_bf = keep.tile([P, P], BF16)
-        nc.vector.tensor_copy(out=ident_bf[:], in_=ident[:])
-        nc.scalar.dma_start(out=bias_rows[0:PACK, :], in_=b_ls.rearrange("(t p) -> t p", p=P))
-        nc.scalar.dma_start(out=bias_rows[PACK : 2 * PACK, :], in_=b_mu.rearrange("(t p) -> t p", p=P))
         lsc_rows = keep.tile([P, PACK, H], BF16)
         muc_rows = keep.tile([P, PACK, H], BF16)
         lsc_dram = log_sigma_sq_c.rearrange("(q r) h -> q r h", r=PACK)
         muc_dram = mu_c.rearrange("(q r) h -> q r h", r=PACK)
-        for g in range(2):
-            nc.sync.dma_start(out=lsc_rows[:, 2 * g : 2 * g + 2, :], in_=lsc_dram[:, 2 * g : 2 * g + 2, :])
-            nc.sync.dma_start(out=muc_rows[:, 2 * g : 2 * g + 2, :], in_=muc_dram[:, 2 * g : 2 * g + 2, :])
         x_rows = keep.tile([P, H], BF16)
-        nc.sync.dma_start(out=x_rows[:], in_=encoder_final_state)
         w_rows = {}
-        for name, w_dram in (("ls", W_ls), ("mu", W_mu)):
+        for name in ("ls", "mu"):
             w_rows[name] = keep.tile([P, PACK, H], BF16, name="w_rows_" + name)
-            nc.sync.dma_start(out=w_rows[name][:], in_=w_dram.rearrange("(t q) k -> q t k", q=P))
         eps_rows = keep.tile([P, H], BF16)
+
+        def load_half(rows, dram, g):
+            nc.sync.dma_start(out=rows[:, 2 * g : 2 * g + 2, :], in_=dram[:, 2 * g : 2 * g + 2, :])
+
+        def load_weight(name, dram):
+            view = dram.rearrange("(u q e) k -> q u e k", u=2, e=2)
+            nc.sync.dma_start(out=w_rows[name][:].rearrange("q (u e) k -> q u e k", e=2), in_=view)
+
+        for g in range(2):
+            load_half(lsc_rows, lsc_dram, g)
+            load_half(muc_rows, muc_dram, g)
+        nc.sync.dma_start(out=x_rows[:], in_=encoder_final_state)
+        nc.sync.dma_start(out=bias_rows[0:1, :], in_=b_ls.rearrange("(a n) -> a n", a=1))
+        nc.sync.dma_start(out=bias_rows[1:2, :], in_=b_mu.rearrange("(a n) -> a n", a=1))
+        load_weight("ls", W_ls)
+        load_weight("mu", W_mu)
         nc.sync.dma_start(out=eps_rows[:], in_=eps_z)
 
-        inv_nat = keep.tile([P, PACK, H], F32)
-        minv_nat = keep.tile([P, PACK, H], F32)
-        prod = keep.tile([P, PACK, H], F32)
+        inv_nat = keep.tile([P, 2, H], F32)
+        minv_nat = keep.tile([P, 2, H], F32)
+        prod_nat = keep.tile([P, 2, H], F32)
+        inv = keep.tile([P, HALF, PACK], F32)
+        muc2 = keep.tile([P, PACK, HALF], F32)
+        prod = keep.tile([P, PACK, HALF], F32)
         c2_col = keep.tile([P, PACK], F32)
-        natural = {"inv": inv_nat, "minv": minv_nat}
         grouped = {}
         codes = {}
         scales = {}
@@ -78,45 +87,109 @@ def tile_latent_pa_s_kernel(
                 in_=grouped[name][:, cols, :].rearrange("p n t -> p (n t)"),
             )
 
-        def cluster_products(r):
-            nc.scalar.activation(out=inv_nat[:, r, :], in_=lsc_rows[:, r, :], func=ACT.Exp, scale=-1.0)
-            nc.vector.tensor_tensor(
-                out=minv_nat[:, r, :], in0=muc_rows[:, r, :], in1=inv_nat[:, r, :], op=ALU.mult
-            )
-
-        def cluster_c2(r):
-            nc.vector.scalar_tensor_tensor(
-                out=prod[:, r, :],
-                in0=minv_nat[:, r, :],
-                scalar=1.0,
-                in1=muc_rows[:, r, :],
-                op0=ALU.mult,
-                op1=ALU.mult,
-                accum_out=c2_col[:, r : r + 1],
-            )
-
-        def cluster_transpose(name, r):
-            bank = psum.tile([P, PACK, P], F32, tag="ct", bufs=3, name="cluster_bank")
-            for t in range(PACK):
-                nc.tensor.transpose(bank[:, t, :], natural[name][:, r, t * P : (t + 1) * P], ident[:])
-            banks[name, r] = bank
-
-        def cluster_round(copy, name, r):
-            copy(
-                out=grouped[name][:, r * P : (r + 1) * P, :],
-                in_=banks[name, r][:].rearrange("p t q -> p q t"),
-            )
-
         def word_transposes(bank_cols, rows):
             words = rows.bitcast(F32)
             for u in range(2):
                 nc.tensor.transpose(bank_cols[:, u, :], words[:, u * P : (u + 1) * P], ident[:])
 
-        def weight_transpose(name, g):
-            bank = psum.tile([P, 2, HALF], F32, tag="wt", name="weight_bank")
+        def transpose_half(name, rows, g):
+            bank = psum.tile([P, 2, HALF], F32, tag="raw", bufs=5, name="raw_bank")
             for i in range(2):
-                word_transposes(bank[:, :, i * P : (i + 1) * P], w_rows[name][:, 2 * g + i, :])
+                word_transposes(bank[:, :, i * P : (i + 1) * P], rows[:, 2 * g + i, :])
             banks[name, g] = bank
+
+        def natural(rows, r):
+            return rows[:, r, :].rearrange("q (n e) -> q e n", e=2)
+
+        def ordered(tile, r):
+            return tile[:, r, :].rearrange("q (e n) -> q e n", e=2)
+
+        def natural_exp(r):
+            nc.scalar.activation(out=ordered(inv_nat, r), in_=natural(lsc_rows, r), func=ACT.Exp, scale=-1.0)
+
+        def natural_minv(r):
+            nc.vector.tensor_tensor(
+                out=ordered(minv_nat, r), in0=natural(muc_rows, r), in1=ordered(inv_nat, r), op=ALU.mult
+            )
+
+        def natural_c2(r):
+            nc.vector.scalar_tensor_tensor(
+                out=ordered(prod_nat, r),
+                in0=ordered(minv_nat, r),
+                scalar=1.0,
+                in1=natural(muc_rows, r),
+                op0=ALU.mult,
+                op1=ALU.mult,
+                accum_out=c2_col[:, r : r + 1],
+            )
+
+        def minv_transpose(r):
+            bank = psum.tile([P, PACK, P], F32, tag="raw", bufs=5, name="minv_bank")
+            for t in range(PACK):
+                first = HALF * (t % 2) + P * (t // 2)
+                nc.tensor.transpose(bank[:, t, :], minv_nat[:, r, first : first + P], ident[:])
+            banks["minv", r] = bank
+
+        def minv_round(copy, r):
+            copy(
+                out=grouped["minv"][:, r * P : (r + 1) * P, :],
+                in_=banks["minv", r][:].rearrange("p t q -> p q t"),
+            )
+
+        def transpose_row(name, rows, r):
+            bank = psum.tile([P, 2, P], F32, tag="raw", bufs=5, name="row_bank")
+            word_transposes(bank[:], rows[:, r, :])
+            banks[name, r, "row"] = bank
+
+        def values(name, r):
+            if name == "muc":
+                both = banks[name, r, "row"][:].bitcast(BF16)
+            else:
+                first = 2 * P * (r % 2)
+                both = banks[name, r // 2][:].bitcast(BF16)[:, :, first : first + 2 * P]
+            return both.rearrange("p u (q e) -> p u q e", e=2)
+
+        def block(tile, r):
+            return tile[:, r * P : (r + 1) * P, :].rearrange("p q (u e) -> p q u e", e=2)
+
+        def transposed_exp(out, r):
+            nc.scalar.activation(
+                out=out, in_=values("lsc", r).rearrange("p u q e -> p q u e"), func=ACT.Exp, scale=-1.0
+            )
+
+        def transposed_square(r):
+            nc.scalar.activation(
+                out=muc2[:, :, (r - 2) * P : (r - 1) * P].rearrange("p (u e) q -> p u e q", e=2),
+                in_=values("muc", r).rearrange("p u q e -> p u e q"),
+                func=ACT.Square,
+            )
+
+        def transposed_minv(r):
+            nc.vector.tensor_tensor(
+                out=block(grouped["minv"], r),
+                in0=values("muc", r).rearrange("p u q e -> p q u e"),
+                in1=block(inv, r - 2),
+                op=ALU.mult,
+            )
+
+        def transposed_prod(r):
+            cols = slice((r - 2) * P, (r - 1) * P)
+            nc.gpsimd.tensor_tensor(
+                out=prod[:, :, cols],
+                in0=muc2[:, :, cols],
+                in1=inv[:, cols, :].rearrange("p q t -> p t q"),
+                op=ALU.mult,
+            )
+
+        def transposed_round(r):
+            nc.gpsimd.tensor_scalar(
+                out=grouped["inv"][:, r * P : (r + 1) * P, :],
+                in0=inv[:, (r - 2) * P : (r - 1) * P, :],
+                scalar1=1.0,
+                scalar2=0.0,
+                op0=ALU.mult,
+                op1=ALU.add,
+            )
 
         def weight_regroup(name, g):
             nc.scalar.copy(
@@ -138,16 +211,37 @@ def tile_latent_pa_s_kernel(
                 )
             return acc
 
-        for r in range(PACK):
-            cluster_products(r)
-        cluster_transpose("inv", 0)
-        cluster_transpose("inv", 1)
-        cluster_transpose("minv", 0)
+        transpose_half("lsc", lsc_rows, 0)
+        for r in (0, 1):
+            natural_exp(r)
+            natural_minv(r)
+        natural_c2(0)
+        transposed_exp(block(grouped["inv"], 0), 0)
+        transpose_half("lsc", lsc_rows, 1)
+        for r in (3, 2):
+            transpose_row("muc", muc_rows, r)
+        for r in (3, 2):
+            transposed_exp(block(inv, r - 2), r)
+            transposed_round(r)
+        transposed_minv(3)
+        natural_c2(1)
+        transposed_exp(block(grouped["inv"], 1), 1)
+        for r in (3, 2):
+            transposed_square(r)
+            transposed_prod(r)
 
-        x_bank = psum.tile([P, 2, B], F32, tag="xe", bufs=1)
-        word_transposes(x_bank[:], x_rows[:])
+        x_bank = psum.tile([P, 2, 2 * P], F32, tag="xe", bufs=1)
+        word_transposes(x_bank[:, :, 0:P], x_rows[:])
+        word_transposes(x_bank[:, :, P : 2 * P], bias_rows[:])
+        bias_values = x_bank[:].bitcast(BF16)[:, :, 2 * P : 2 * P + 4]
+        half_bls = keep.tile([P, 2, 2], F32)
+        bmu = keep.tile([P, 2, 2], F32)
         x_grouped = keep.tile([P, B, PACK], BF16, align_bytes=64)
-        nc.vector.tensor_copy(out=x_grouped[:].bitcast(F32), in_=x_bank[:].rearrange("p u n -> p n u"))
+        nc.vector.tensor_copy(
+            out=x_grouped[:].bitcast(F32), in_=x_bank[:, :, 0:P].rearrange("p u n -> p n u")
+        )
+        nc.vector.tensor_scalar_mul(out=half_bls[:], in0=bias_values[:, :, 0:2], scalar1=0.5)
+        nc.vector.tensor_copy(out=bmu[:], in_=bias_values[:, :, 2:4])
         x_codes = keep.tile([P, B], U32, align_bytes=64)
         x_scales = keep.tile([P, B], U8, align_bytes=64)
         nc.vector.quantize_mx(
@@ -155,134 +249,129 @@ def tile_latent_pa_s_kernel(
             scales=x_scales[:],
             in_=x_grouped[:].rearrange("p n t -> p (n t)"),
         )
-
-        cluster_round(nc.scalar.copy, "inv", 0)
-        cluster_round(nc.scalar.copy, "inv", 1)
-        cluster_round(nc.scalar.copy, "minv", 0)
-        cluster_c2(0)
-        cluster_c2(1)
-
-        weight_transpose("ls", 0)
-        weight_transpose("ls", 1)
-        cluster_transpose("minv", 1)
-        weight_regroup("ls", 0)
-        weight_regroup("ls", 1)
-        cluster_round(nc.vector.tensor_copy, "minv", 1)
-        quantise_half("ls", 0)
-        quantise_half("ls", 1)
-        cluster_c2(2)
-        weight_transpose("mu", 0)
-        weight_transpose("mu", 1)
-        weight_regroup("mu", 0)
-        weight_regroup("mu", 1)
-        quantise_half("mu", 0)
-        quantise_half("mu", 1)
-
-        eb_bank = psum.tile([P, PACK + 1, P], BF16, tag="xe", bufs=1)
-        for t in range(PACK):
-            nc.tensor.transpose(eb_bank[:, t, :], eps_rows[:, t * P : (t + 1) * P], ident_bf[:])
-        nc.tensor.transpose(eb_bank[:, PACK, :], bias_rows[:], ident_bf[:])
-        half_bls = keep.tile([P, PACK], F32)
-        bmu = keep.tile([P, PACK], F32)
-        nc.vector.tensor_scalar_mul(out=half_bls[:], in0=eb_bank[:, PACK, 0:PACK], scalar1=0.5)
-        nc.vector.tensor_copy(out=bmu[:], in_=eb_bank[:, PACK, PACK : 2 * PACK])
-
-        cluster_transpose("inv", 2)
-        cluster_transpose("inv", 3)
-        ls_acc = first_product("ls")
-        cluster_round(nc.scalar.copy, "inv", 2)
-        cluster_transpose("minv", 2)
-        mu_acc = first_product("mu")
-        cluster_transpose("minv", 3)
-        cluster_c2(3)
-
-        c2_bank = psum.tile([P, C], F32, tag="wt")
-        for r in range(PACK):
-            nc.tensor.matmul(
-                out=c2_bank[:, r * P : (r + 1) * P],
-                lhsT=c2_col[:, r : r + 1].to_broadcast([P, P]),
-                rhs=ident[:],
-                start=True,
-                stop=True,
-            )
+        quantise_half("inv", 1)
+        transposed_minv(2)
         quantise_half("inv", 0)
-        quantise_half("minv", 0)
+        for g in range(2):
+            transpose_half("ls", w_rows["ls"], g)
+            weight_regroup("ls", g)
+            quantise_half("ls", g)
+        quantise_half("minv", 1)
+        for g in range(2):
+            transpose_half("mu", w_rows["mu"], g)
+            weight_regroup("mu", g)
+            quantise_half("mu", g)
+        eb_bank = psum.tile([P, 2, P], F32, tag="xe", bufs=1)
+        word_transposes(eb_bank[:], eps_rows[:])
+        eb_values = eb_bank[:].bitcast(BF16)
+        minv_transpose(0)
+        minv_transpose(1)
+        ls_acc = first_product("ls")
+        mu_acc = first_product("mu")
+        part_bank = psum.tile([P, 2, P], F32, tag="raw", bufs=5)
+
+        def c2_transposes(r):
+            for t in range(PACK):
+                nc.tensor.matmul(
+                    out=part_bank[:, r - 2, :],
+                    lhsT=prod[:, t, (r - 2) * P : (r - 1) * P],
+                    rhs=ident[:],
+                    start=t == 0,
+                    stop=t == PACK - 1,
+                    is_transpose=True,
+                )
+
+        c2_transposes(3)
+        c2_transposes(2)
 
         s_sb = keep.tile([P, PACK, B], F32)
         w_sb = keep.tile([P, PACK, B], F32)
         z_sb = keep.tile([P, PACK, B], F32)
-        z_bank = psum.tile([P, PACK, P], F32, tag="wt")
+        z_bank = psum.tile([P, PACK, P], F32, tag="raw", bufs=5)
         for t in range(PACK):
             nc.scalar.activation(
-                out=s_sb[:, t, :], in_=ls_acc[:, t, :], func=ACT.Exp, bias=half_bls[:, t : t + 1], scale=0.5
+                out=s_sb[:, t, :],
+                in_=ls_acc[:, t, :],
+                func=ACT.Exp,
+                bias=half_bls[:, t // 2, t % 2 : t % 2 + 1],
+                scale=0.5,
             )
 
         def scaled_noise(t):
-            nc.vector.tensor_tensor(out=w_sb[:, t, :], in0=s_sb[:, t, :], in1=eb_bank[:, t, :], op=ALU.mult)
+            eps_t = eb_values[:, t // 2, 0 : 2 * P].rearrange("p (b e) -> p e b", e=2)[:, t % 2, :]
+            nc.vector.tensor_tensor(out=w_sb[:, t, :], in0=s_sb[:, t, :], in1=eps_t, op=ALU.mult)
 
         def latent(t):
             nc.vector.scalar_tensor_tensor(
                 out=z_sb[:, t, :],
                 in0=mu_acc[:, t, :],
-                scalar=bmu[:, t : t + 1],
+                scalar=bmu[:, t // 2, t % 2 : t % 2 + 1],
                 in1=w_sb[:, t, :],
                 op0=ALU.add,
                 op1=ALU.add,
             )
             nc.tensor.transpose(z_bank[:, t, :], z_sb[:, t, :], ident[:])
 
+        minv_round(nc.scalar.copy, 0)
+        minv_round(nc.scalar.copy, 1)
         scaled_noise(0)
         for t in range(1, PACK):
             scaled_noise(t)
             latent(t - 1)
         latent(PACK - 1)
-
-        cluster_round(nc.scalar.copy, "inv", 3)
-        cluster_round(nc.scalar.copy, "minv", 2)
-        cluster_round(nc.scalar.copy, "minv", 3)
-        quantise_half("inv", 1)
+        nc.vector.tensor_reduce(out=c2_col[:, 2:4], in_=part_bank[:], axis=AX.X, op=ALU.add)
 
         z_grouped = keep.tile([P, 2, B, PACK], BF16, align_bytes=64)
         z_view = z_sb[:].rearrange("p t b -> p b t")
         nc.vector.tensor_scalar_mul(out=z_grouped[:, 0, :, :], in0=z_view, scalar1=-2.0)
         nc.scalar.activation(out=z_grouped[:, 1, :, :], in_=z_view, func=ACT.Square)
-        quantise_half("minv", 1)
+        quantise_half("minv", 0)
         z_codes = keep.tile([P, 2 * B], U32, align_bytes=64)
         z_scales = keep.tile([P, 2 * B], U8, align_bytes=64)
-        nc.vector.quantize_mx(
-            out=z_codes[:].bitcast(FP8X4),
-            scales=z_scales[:],
-            in_=z_grouped[:].rearrange("p a b t -> p (a b t)"),
-        )
+        for a in range(2):
+            nc.vector.quantize_mx(
+                out=z_codes[:, a * B : (a + 1) * B].bitcast(FP8X4),
+                scales=z_scales[:, a * B : (a + 1) * B],
+                in_=z_grouped[:, a, :, :].rearrange("p b t -> p (b t)"),
+            )
+        c2_bank = psum.tile([P, C], F32, tag="s1")
+        for r in range(PACK):
+            nc.tensor.transpose(
+                c2_bank[:, r * P : (r + 1) * P], c2_col[:, r : r + 1].to_broadcast([P, P]), ident[:]
+            )
         c2_sb = keep.tile([P, C], F32)
         nc.scalar.copy(out=c2_sb[:], in_=c2_bank[:])
 
         z_out = keep.tile([P, H], F32)
-        nc.scalar.copy(out=z_out[:], in_=z_bank[:].rearrange("b t p -> b (t p)"))
+        nc.scalar.copy(
+            out=z_out[:].rearrange("b (u p e) -> b u p e", u=2, e=2),
+            in_=z_bank[:].rearrange("b (u e) p -> b u p e", e=2),
+        )
         nc.sync.dma_start(out=out_0, in_=z_out[:])
 
-        d_bank = psum.tile([P, C], F32, tag="ct", bufs=3)
-        nc.tensor.matmul_mx(
-            out=d_bank[:],
-            lhsT=z_codes[:, B : 2 * B].bitcast(FP8X4),
-            lhsT_scale=z_scales[:, B : 2 * B],
-            rhs=codes["inv"][:].bitcast(FP8X4),
-            rhs_scale=scales["inv"][:],
-            start=True,
-            stop=False,
-        )
-        nc.tensor.matmul_mx(
-            out=d_bank[:],
-            lhsT=z_codes[:, 0:B].bitcast(FP8X4),
-            lhsT_scale=z_scales[:, 0:B],
-            rhs=codes["minv"][:].bitcast(FP8X4),
-            rhs_scale=scales["minv"][:],
-            start=False,
-            stop=True,
-        )
-        d_sb = keep.tile([P, C], F32)
-        nc.vector.tensor_tensor(out=d_sb[:], in0=d_bank[:], in1=c2_sb[:], op=ALU.add)
+        d_banks = [psum.tile([P, HALF], F32, tag="raw", bufs=5, name="d_bank") for g in range(2)]
 
+        def second_product(a, name, start, g):
+            cols = slice(g * HALF, (g + 1) * HALF)
+            nc.tensor.matmul_mx(
+                out=d_banks[g][:],
+                lhsT=z_codes[:, a * B : (a + 1) * B].bitcast(FP8X4),
+                lhsT_scale=z_scales[:, a * B : (a + 1) * B],
+                rhs=codes[name][:, cols].bitcast(FP8X4),
+                rhs_scale=scales[name][:, cols],
+                start=start,
+                stop=not start,
+            )
+
+        for g in range(2):
+            second_product(0, "minv", True, g)
+        for g in range(2):
+            second_product(1, "inv", False, g)
+
+        d_sb = keep.tile([P, C], F32)
+        for g in range(2):
+            cols = slice(g * HALF, (g + 1) * HALF)
+            nc.vector.tensor_tensor(out=d_sb[:, cols], in0=d_banks[g][:], in1=c2_sb[:, cols], op=ALU.add)
         d_min = keep.tile([P, 1], F32)
         nc.vector.tensor_reduce(out=d_min[:], in_=d_sb[:], axis=AX.X, op=ALU.min)
         e_sb = keep.tile([P, C], F32)

@@ -46,29 +46,32 @@ def tile_latent_pa_s_kernel(
             w_rows[name] = keep.tile([P, PACK, H], BF16, name="w_rows_" + name)
         eps_rows = keep.tile([P, H], BF16)
 
-        def load_half(rows, dram, g):
-            nc.sync.dma_start(out=rows[:, 2 * g : 2 * g + 2, :], in_=dram[:, 2 * g : 2 * g + 2, :])
+        def load_rows(rows, dram, first, last):
+            nc.sync.dma_start(out=rows[:, first:last, :], in_=dram[:, first:last, :])
 
         def load_weight(name, dram):
             view = dram.rearrange("(u q e) k -> q u e k", u=2, e=2)
             nc.sync.dma_start(out=w_rows[name][:].rearrange("q (u e) k -> q u e k", e=2), in_=view)
 
-        for g in range(2):
-            load_half(lsc_rows, lsc_dram, g)
-            load_half(muc_rows, muc_dram, g)
+        load_rows(lsc_rows, lsc_dram, 0, 1)
+        load_rows(muc_rows, muc_dram, 0, 1)
+        load_rows(lsc_rows, lsc_dram, 1, 2)
+        load_rows(lsc_rows, lsc_dram, 2, PACK)
+        load_rows(muc_rows, muc_dram, 1, 2)
+        load_rows(muc_rows, muc_dram, 2, PACK)
         nc.sync.dma_start(out=x_rows[:], in_=encoder_final_state)
-        nc.sync.dma_start(out=bias_rows[0:1, :], in_=b_ls.rearrange("(a n) -> a n", a=1))
-        nc.sync.dma_start(out=bias_rows[1:2, :], in_=b_mu.rearrange("(a n) -> a n", a=1))
         load_weight("ls", W_ls)
         load_weight("mu", W_mu)
         nc.sync.dma_start(out=eps_rows[:], in_=eps_z)
+        nc.scalar.dma_start(out=bias_rows[0:1, :], in_=b_ls.rearrange("(a n) -> a n", a=1))
+        nc.scalar.dma_start(out=bias_rows[1:2, :], in_=b_mu.rearrange("(a n) -> a n", a=1))
 
-        inv_nat = keep.tile([P, 2, H], F32)
-        minv_nat = keep.tile([P, 2, H], F32)
-        prod_nat = keep.tile([P, 2, H], F32)
-        inv = keep.tile([P, HALF, PACK], F32)
-        muc2 = keep.tile([P, PACK, HALF], F32)
-        prod = keep.tile([P, PACK, HALF], F32)
+        inv_nat = keep.tile([P, H], F32)
+        minv_nat = keep.tile([P, H], F32)
+        prod_nat = keep.tile([P, H], F32)
+        inv = keep.tile([P, PACK, C], F32)
+        minv = keep.tile([P, PACK, C], F32)
+        prod = keep.tile([P, PACK, C], F32)
         c2_col = keep.tile([P, PACK], F32)
         grouped = {}
         codes = {}
@@ -93,98 +96,96 @@ def tile_latent_pa_s_kernel(
                 nc.tensor.transpose(bank_cols[:, u, :], words[:, u * P : (u + 1) * P], ident[:])
 
         def transpose_half(name, rows, g):
-            bank = psum.tile([P, 2, HALF], F32, tag="raw", bufs=5, name="raw_bank")
+            if (name, g) == ("lsc", 0):
+                bank = psum.tile([P, 2, HALF], F32, tag="s1", name="first_bank")
+            elif name == "muc":
+                bank = psum.tile([P, 2, HALF], F32, tag="mc", bufs=1, name="muc_bank")
+            else:
+                bank = psum.tile([P, 2, HALF], F32, tag="raw", bufs=4, name="raw_bank")
             for i in range(2):
                 word_transposes(bank[:, :, i * P : (i + 1) * P], rows[:, 2 * g + i, :])
             banks[name, g] = bank
 
-        def natural(rows, r):
-            return rows[:, r, :].rearrange("q (n e) -> q e n", e=2)
+        def transpose_row(name, rows, r):
+            bank = psum.tile([P, 2, HALF], F32, tag="raw", bufs=4, name="row_bank")
+            word_transposes(bank[:, :, (r % 2) * P : (r % 2 + 1) * P], rows[:, r, :])
+            banks[name, r // 2] = bank
 
-        def ordered(tile, r):
-            return tile[:, r, :].rearrange("q (e n) -> q e n", e=2)
+        natural_lsc = lsc_rows[:, 0, :].rearrange("q (n e) -> q e n", e=2)
+        natural_muc = muc_rows[:, 0, :].rearrange("q (n e) -> q e n", e=2)
 
-        def natural_exp(r):
-            nc.scalar.activation(out=ordered(inv_nat, r), in_=natural(lsc_rows, r), func=ACT.Exp, scale=-1.0)
+        def ordered(tile):
+            return tile[:].rearrange("q (e n) -> q e n", e=2)
 
-        def natural_minv(r):
-            nc.vector.tensor_tensor(
-                out=ordered(minv_nat, r), in0=natural(muc_rows, r), in1=ordered(inv_nat, r), op=ALU.mult
-            )
+        def natural_exp():
+            nc.scalar.activation(out=ordered(inv_nat), in_=natural_lsc, func=ACT.Exp, scale=-1.0)
 
-        def natural_c2(r):
+        def natural_minv():
+            nc.vector.tensor_tensor(out=ordered(minv_nat), in0=natural_muc, in1=ordered(inv_nat), op=ALU.mult)
+
+        def natural_c2():
             nc.vector.scalar_tensor_tensor(
-                out=ordered(prod_nat, r),
-                in0=ordered(minv_nat, r),
+                out=ordered(prod_nat),
+                in0=ordered(minv_nat),
                 scalar=1.0,
-                in1=natural(muc_rows, r),
+                in1=natural_muc,
                 op0=ALU.mult,
                 op1=ALU.mult,
-                accum_out=c2_col[:, r : r + 1],
+                accum_out=c2_col[:, 0:1],
             )
 
-        def minv_transpose(r):
-            bank = psum.tile([P, PACK, P], F32, tag="raw", bufs=5, name="minv_bank")
+        def minv_transpose():
+            bank = psum.tile([P, PACK, P], F32, tag="s1", name="minv_bank")
             for t in range(PACK):
                 first = HALF * (t % 2) + P * (t // 2)
-                nc.tensor.transpose(bank[:, t, :], minv_nat[:, r, first : first + P], ident[:])
-            banks["minv", r] = bank
+                nc.tensor.transpose(bank[:, t, :], minv_nat[:, first : first + P], ident[:])
+            banks["minv"] = bank
 
-        def minv_round(copy, r):
-            copy(
-                out=grouped["minv"][:, r * P : (r + 1) * P, :],
-                in_=banks["minv", r][:].rearrange("p t q -> p q t"),
-            )
-
-        def transpose_row(name, rows, r):
-            bank = psum.tile([P, 2, P], F32, tag="raw", bufs=5, name="row_bank")
-            word_transposes(bank[:], rows[:, r, :])
-            banks[name, r, "row"] = bank
+        def minv_round(copy):
+            copy(out=grouped["minv"][:, 0:P, :], in_=banks["minv"][:].rearrange("p t q -> p q t"))
 
         def values(name, r):
-            if name == "muc":
-                both = banks[name, r, "row"][:].bitcast(BF16)
-            else:
-                first = 2 * P * (r % 2)
-                both = banks[name, r // 2][:].bitcast(BF16)[:, :, first : first + 2 * P]
+            first = 2 * P * (r % 2)
+            both = banks[name, r // 2][:].bitcast(BF16)[:, :, first : first + 2 * P]
             return both.rearrange("p u (q e) -> p u q e", e=2)
 
-        def block(tile, r):
-            return tile[:, r * P : (r + 1) * P, :].rearrange("p q (u e) -> p q u e", e=2)
+        def quarter(tile, r):
+            return tile[:, :, r * P : (r + 1) * P].rearrange("p (u e) q -> p u e q", e=2)
 
-        def transposed_exp(out, r):
+        def inverse_exp(r):
             nc.scalar.activation(
-                out=out, in_=values("lsc", r).rearrange("p u q e -> p q u e"), func=ACT.Exp, scale=-1.0
+                out=grouped["inv"][:, r * P : (r + 1) * P, :].rearrange("p q (u e) -> p q u e", e=2),
+                in_=values("lsc", r).rearrange("p u q e -> p q u e"),
+                func=ACT.Exp,
+                scale=-1.0,
             )
 
-        def transposed_square(r):
+        def cluster_exp(r):
             nc.scalar.activation(
-                out=muc2[:, :, (r - 2) * P : (r - 1) * P].rearrange("p (u e) q -> p u e q", e=2),
-                in_=values("muc", r).rearrange("p u q e -> p u e q"),
-                func=ACT.Square,
+                out=quarter(inv, r), in_=values("lsc", r).rearrange("p u q e -> p u e q"), func=ACT.Exp, scale=-1.0
             )
 
-        def transposed_minv(r):
+        def cluster_minv(r):
             nc.vector.tensor_tensor(
-                out=block(grouped["minv"], r),
-                in0=values("muc", r).rearrange("p u q e -> p q u e"),
-                in1=block(inv, r - 2),
+                out=quarter(minv, r),
+                in0=values("muc", r).rearrange("p u q e -> p u e q"),
+                in1=quarter(inv, r),
                 op=ALU.mult,
             )
 
-        def transposed_prod(r):
-            cols = slice((r - 2) * P, (r - 1) * P)
-            nc.gpsimd.tensor_tensor(
-                out=prod[:, :, cols],
-                in0=muc2[:, :, cols],
-                in1=inv[:, cols, :].rearrange("p q t -> p t q"),
+        def cluster_prod(r):
+            nc.vector.tensor_tensor(
+                out=quarter(prod, r),
+                in0=values("muc", r).rearrange("p u q e -> p u e q"),
+                in1=quarter(minv, r),
                 op=ALU.mult,
             )
 
-        def transposed_round(r):
+        def cluster_round(name, tile, r):
+            cols = slice(r * P, (r + 1) * P)
             nc.gpsimd.tensor_scalar(
-                out=grouped["inv"][:, r * P : (r + 1) * P, :],
-                in0=inv[:, (r - 2) * P : (r - 1) * P, :],
+                out=grouped[name][:, cols, :],
+                in0=tile[:, :, cols].rearrange("p t q -> p q t"),
                 scalar1=1.0,
                 scalar2=0.0,
                 op0=ALU.mult,
@@ -197,8 +198,7 @@ def tile_latent_pa_s_kernel(
                 in_=banks[name, g][:].rearrange("p u n -> p n u"),
             )
 
-        def first_product(name):
-            acc = psum.tile([P, PACK, B], F32, tag="s1", name="s1_" + name)
+        def first_product(name, acc):
             for t in range(PACK):
                 nc.tensor.matmul_mx(
                     out=acc[:, t, :],
@@ -209,85 +209,96 @@ def tile_latent_pa_s_kernel(
                     start=True,
                     stop=True,
                 )
-            return acc
 
         transpose_half("lsc", lsc_rows, 0)
-        for r in (0, 1):
-            natural_exp(r)
-            natural_minv(r)
-        natural_c2(0)
-        transposed_exp(block(grouped["inv"], 0), 0)
+        natural_exp()
+        natural_minv()
+        natural_c2()
+        cluster_exp(1)
+        cluster_round("inv", inv, 1)
+        inverse_exp(0)
         transpose_half("lsc", lsc_rows, 1)
-        for r in (3, 2):
-            transpose_row("muc", muc_rows, r)
-        for r in (3, 2):
-            transposed_exp(block(inv, r - 2), r)
-            transposed_round(r)
-        transposed_minv(3)
-        natural_c2(1)
-        transposed_exp(block(grouped["inv"], 1), 1)
-        for r in (3, 2):
-            transposed_square(r)
-            transposed_prod(r)
+        transpose_row("muc", muc_rows, 1)
+        transpose_half("muc", muc_rows, 1)
+        cluster_exp(2)
+        cluster_round("inv", inv, 2)
+        cluster_exp(3)
+        inverse_exp(3)
+        cluster_minv(1)
+        cluster_minv(2)
+        cluster_round("minv", minv, 1)
+        cluster_round("minv", minv, 2)
+        cluster_prod(1)
 
-        x_bank = psum.tile([P, 2, 2 * P], F32, tag="xe", bufs=1)
-        word_transposes(x_bank[:, :, 0:P], x_rows[:])
-        word_transposes(x_bank[:, :, P : 2 * P], bias_rows[:])
-        bias_values = x_bank[:].bitcast(BF16)[:, :, 2 * P : 2 * P + 4]
-        half_bls = keep.tile([P, 2, 2], F32)
-        bmu = keep.tile([P, 2, 2], F32)
+        x_bank = psum.tile([P, 2, B], F32, tag="xe", bufs=1)
+        word_transposes(x_bank[:], x_rows[:])
         x_grouped = keep.tile([P, B, PACK], BF16, align_bytes=64)
-        nc.vector.tensor_copy(
-            out=x_grouped[:].bitcast(F32), in_=x_bank[:, :, 0:P].rearrange("p u n -> p n u")
-        )
-        nc.vector.tensor_scalar_mul(out=half_bls[:], in0=bias_values[:, :, 0:2], scalar1=0.5)
-        nc.vector.tensor_copy(out=bmu[:], in_=bias_values[:, :, 2:4])
+        nc.scalar.copy(out=x_grouped[:].bitcast(F32), in_=x_bank[:].rearrange("p u n -> p n u"))
         x_codes = keep.tile([P, B], U32, align_bytes=64)
         x_scales = keep.tile([P, B], U8, align_bytes=64)
+        cluster_minv(3)
+        cluster_round("minv", minv, 3)
+        cluster_prod(2)
+        cluster_prod(3)
         nc.vector.quantize_mx(
             out=x_codes[:].bitcast(FP8X4),
             scales=x_scales[:],
             in_=x_grouped[:].rearrange("p n t -> p (n t)"),
         )
-        quantise_half("inv", 1)
-        transposed_minv(2)
-        quantise_half("inv", 0)
         for g in range(2):
             transpose_half("ls", w_rows["ls"], g)
             weight_regroup("ls", g)
             quantise_half("ls", g)
-        quantise_half("minv", 1)
         for g in range(2):
             transpose_half("mu", w_rows["mu"], g)
             weight_regroup("mu", g)
             quantise_half("mu", g)
-        eb_bank = psum.tile([P, 2, P], F32, tag="xe", bufs=1)
-        word_transposes(eb_bank[:], eps_rows[:])
+        eb_bank = psum.tile([P, 2, 2 * P], F32, tag="xe", bufs=1)
+        word_transposes(eb_bank[:, :, 0:P], eps_rows[:])
+        word_transposes(eb_bank[:, :, P : 2 * P], bias_rows[:])
         eb_values = eb_bank[:].bitcast(BF16)
-        minv_transpose(0)
-        minv_transpose(1)
-        ls_acc = first_product("ls")
-        mu_acc = first_product("mu")
-        part_bank = psum.tile([P, 2, P], F32, tag="raw", bufs=5)
-
+        half_bls = keep.tile([P, 2, 2], F32)
+        bmu = keep.tile([P, 2, 2], F32)
+        nc.vector.tensor_scalar_mul(out=half_bls[:], in0=eb_values[:, :, 2 * P : 2 * P + 2], scalar1=0.5)
+        nc.vector.tensor_copy(out=bmu[:], in_=eb_values[:, :, 2 * P + 2 : 2 * P + 4])
+        quantise_half("inv", 0)
+        quantise_half("inv", 1)
         def c2_transposes(r):
+            if r == 1:
+                bank = psum.tile([P, P], F32, tag="mc", bufs=1, name="part_bank")
+            else:
+                bank = psum.tile([P, P], F32, tag="raw", bufs=4, name="part_bank")
             for t in range(PACK):
                 nc.tensor.matmul(
-                    out=part_bank[:, r - 2, :],
-                    lhsT=prod[:, t, (r - 2) * P : (r - 1) * P],
+                    out=bank[:],
+                    lhsT=prod[:, t, r * P : (r + 1) * P],
                     rhs=ident[:],
                     start=t == 0,
                     stop=t == PACK - 1,
                     is_transpose=True,
                 )
+            banks["part", r] = bank
 
-        c2_transposes(3)
-        c2_transposes(2)
+        def c2_sum(r):
+            nc.scalar.activation(
+                out=part_scratch[:, r, :], in_=banks["part", r][:], func=ACT.Copy, accum_out=c2_col[:, r : r + 1]
+            )
+
+        part_scratch = keep.tile([P, PACK, P], F32)
+
+        ls_acc = psum.tile([P, PACK, B], F32, tag="s1", name="ls_acc")
+        minv_transpose()
+        minv_round(nc.scalar.copy)
+        first_product("ls", ls_acc)
+        mu_acc = psum.tile([P, PACK, B], F32, tag="raw", bufs=4, name="mu_acc")
+        first_product("mu", mu_acc)
+        for r in range(1, PACK):
+            c2_transposes(r)
 
         s_sb = keep.tile([P, PACK, B], F32)
         w_sb = keep.tile([P, PACK, B], F32)
         z_sb = keep.tile([P, PACK, B], F32)
-        z_bank = psum.tile([P, PACK, P], F32, tag="raw", bufs=5)
+        z_bank = psum.tile([P, PACK, P], F32, tag="raw", bufs=4)
         for t in range(PACK):
             nc.scalar.activation(
                 out=s_sb[:, t, :],
@@ -312,20 +323,23 @@ def tile_latent_pa_s_kernel(
             )
             nc.tensor.transpose(z_bank[:, t, :], z_sb[:, t, :], ident[:])
 
-        minv_round(nc.scalar.copy, 0)
-        minv_round(nc.scalar.copy, 1)
         scaled_noise(0)
-        for t in range(1, PACK):
-            scaled_noise(t)
-            latent(t - 1)
-        latent(PACK - 1)
-        nc.vector.tensor_reduce(out=c2_col[:, 2:4], in_=part_bank[:], axis=AX.X, op=ALU.add)
+        scaled_noise(1)
+        latent(0)
+        scaled_noise(2)
+        latent(1)
+        scaled_noise(3)
+        latent(2)
+        latent(3)
+        for r in range(1, PACK):
+            c2_sum(r)
+        quantise_half("minv", 0)
 
         z_grouped = keep.tile([P, 2, B, PACK], BF16, align_bytes=64)
         z_view = z_sb[:].rearrange("p t b -> p b t")
         nc.vector.tensor_scalar_mul(out=z_grouped[:, 0, :, :], in0=z_view, scalar1=-2.0)
         nc.scalar.activation(out=z_grouped[:, 1, :, :], in_=z_view, func=ACT.Square)
-        quantise_half("minv", 0)
+        quantise_half("minv", 1)
         z_codes = keep.tile([P, 2 * B], U32, align_bytes=64)
         z_scales = keep.tile([P, 2 * B], U8, align_bytes=64)
         for a in range(2):
@@ -349,7 +363,7 @@ def tile_latent_pa_s_kernel(
         )
         nc.sync.dma_start(out=out_0, in_=z_out[:])
 
-        d_banks = [psum.tile([P, HALF], F32, tag="raw", bufs=5, name="d_bank") for g in range(2)]
+        d_banks = [psum.tile([P, HALF], F32, tag="raw", bufs=4, name="d_bank") for g in range(2)]
 
         def second_product(a, name, start, g):
             cols = slice(g * HALF, (g + 1) * HALF)

@@ -63,8 +63,8 @@ def tile_latent_pa_s_kernel(
         load_weight("ls", W_ls)
         load_weight("mu", W_mu)
         nc.sync.dma_start(out=eps_rows[:], in_=eps_z)
-        nc.scalar.dma_start(out=bias_rows[0:1, :], in_=b_ls.rearrange("(a n) -> a n", a=1))
-        nc.scalar.dma_start(out=bias_rows[1:2, :], in_=b_mu.rearrange("(a n) -> a n", a=1))
+        nc.sync.dma_start(out=bias_rows[0:1, :], in_=b_ls.rearrange("(a n) -> a n", a=1))
+        nc.sync.dma_start(out=bias_rows[1:2, :], in_=b_mu.rearrange("(a n) -> a n", a=1))
 
         inv_nat = keep.tile([P, H], F32)
         minv_nat = keep.tile([P, H], F32)
@@ -216,13 +216,13 @@ def tile_latent_pa_s_kernel(
         natural_c2()
         cluster_exp(1)
         cluster_round("inv", inv, 1)
-        inverse_exp(0)
         transpose_half("lsc", lsc_rows, 1)
         transpose_row("muc", muc_rows, 1)
         transpose_half("muc", muc_rows, 1)
         cluster_exp(2)
         cluster_round("inv", inv, 2)
         cluster_exp(3)
+        inverse_exp(0)
         inverse_exp(3)
         cluster_minv(1)
         cluster_minv(2)
@@ -236,10 +236,10 @@ def tile_latent_pa_s_kernel(
         nc.scalar.copy(out=x_grouped[:].bitcast(F32), in_=x_bank[:].rearrange("p u n -> p n u"))
         x_codes = keep.tile([P, B], U32, align_bytes=64)
         x_scales = keep.tile([P, B], U8, align_bytes=64)
+        minv_transpose()
         cluster_minv(3)
         cluster_round("minv", minv, 3)
         cluster_prod(2)
-        cluster_prod(3)
         nc.vector.quantize_mx(
             out=x_codes[:].bitcast(FP8X4),
             scales=x_scales[:],
@@ -249,22 +249,24 @@ def tile_latent_pa_s_kernel(
             transpose_half("ls", w_rows["ls"], g)
             weight_regroup("ls", g)
             quantise_half("ls", g)
+        cluster_prod(3)
         for g in range(2):
             transpose_half("mu", w_rows["mu"], g)
             weight_regroup("mu", g)
             quantise_half("mu", g)
+        minv_round(nc.scalar.copy)
         eb_bank = psum.tile([P, 2, 2 * P], F32, tag="xe", bufs=1)
         word_transposes(eb_bank[:, :, 0:P], eps_rows[:])
         word_transposes(eb_bank[:, :, P : 2 * P], bias_rows[:])
         eb_values = eb_bank[:].bitcast(BF16)
         half_bls = keep.tile([P, 2, 2], F32)
         bmu = keep.tile([P, 2, 2], F32)
-        nc.vector.tensor_scalar_mul(out=half_bls[:], in0=eb_values[:, :, 2 * P : 2 * P + 2], scalar1=0.5)
-        nc.vector.tensor_copy(out=bmu[:], in_=eb_values[:, :, 2 * P + 2 : 2 * P + 4])
+        nc.scalar.mul(half_bls[:], eb_values[:, :, 2 * P : 2 * P + 2], 0.5)
+        nc.scalar.copy(out=bmu[:], in_=eb_values[:, :, 2 * P + 2 : 2 * P + 4])
         quantise_half("inv", 0)
         quantise_half("inv", 1)
         def c2_transposes(r):
-            if r == 1:
+            if r == PACK - 1:
                 bank = psum.tile([P, P], F32, tag="mc", bufs=1, name="part_bank")
             else:
                 bank = psum.tile([P, P], F32, tag="raw", bufs=4, name="part_bank")
@@ -286,14 +288,14 @@ def tile_latent_pa_s_kernel(
 
         part_scratch = keep.tile([P, PACK, P], F32)
 
+        c2_transposes(1)
+        c2_sum(1)
         ls_acc = psum.tile([P, PACK, B], F32, tag="s1", name="ls_acc")
-        minv_transpose()
-        minv_round(nc.scalar.copy)
         first_product("ls", ls_acc)
         mu_acc = psum.tile([P, PACK, B], F32, tag="raw", bufs=4, name="mu_acc")
         first_product("mu", mu_acc)
-        for r in range(1, PACK):
-            c2_transposes(r)
+        c2_transposes(2)
+        c2_transposes(3)
 
         s_sb = keep.tile([P, PACK, B], F32)
         w_sb = keep.tile([P, PACK, B], F32)
@@ -331,7 +333,7 @@ def tile_latent_pa_s_kernel(
         scaled_noise(3)
         latent(2)
         latent(3)
-        for r in range(1, PACK):
+        for r in (2, 3):
             c2_sum(r)
         quantise_half("minv", 0)
 

@@ -34,12 +34,12 @@ def tile_latent_pa_s_kernel(
         ident = keep.tile([P, P], F32)
         make_identity(nc, ident[:])
 
-        bias_rows = keep.tile([P, H], BF16)
-        nc.vector.memset(bias_rows[:], 0.0)
+        bls = keep.tile([P, 2, 2], BF16)
+        bmu = keep.tile([P, 2, 2], BF16)
         lsc_rows = keep.tile([P, PACK, H], BF16)
         muc_rows = keep.tile([P, PACK, H], BF16)
-        lsc_dram = log_sigma_sq_c.rearrange("(q r) h -> q r h", r=PACK)
-        muc_dram = mu_c.rearrange("(q r) h -> q r h", r=PACK)
+        lsc_dram = log_sigma_sq_c.rearrange("(r q) h -> q r h", r=PACK)
+        muc_dram = mu_c.rearrange("(r q) h -> q r h", r=PACK)
         x_rows = keep.tile([P, H], BF16)
         w_rows = {}
         for name in ("ls", "mu"):
@@ -53,25 +53,22 @@ def tile_latent_pa_s_kernel(
             view = dram.rearrange("(u q e) k -> q u e k", u=2, e=2)
             nc.sync.dma_start(out=w_rows[name][:].rearrange("q (u e) k -> q u e k", e=2), in_=view)
 
-        load_rows(lsc_rows, lsc_dram, 0, 1)
-        load_rows(muc_rows, muc_dram, 0, 1)
-        load_rows(lsc_rows, lsc_dram, 1, 2)
-        load_rows(lsc_rows, lsc_dram, 2, PACK)
-        load_rows(muc_rows, muc_dram, 1, 2)
-        load_rows(muc_rows, muc_dram, 2, PACK)
+        for first, last in ((0, 1), (1, 2), (2, PACK)):
+            load_rows(lsc_rows, lsc_dram, first, last)
+            load_rows(muc_rows, muc_dram, first, last)
         nc.sync.dma_start(out=x_rows[:], in_=encoder_final_state)
         load_weight("ls", W_ls)
         load_weight("mu", W_mu)
         nc.sync.dma_start(out=eps_rows[:], in_=eps_z)
-        nc.sync.dma_start(out=bias_rows[0:1, :], in_=b_ls.rearrange("(a n) -> a n", a=1))
-        nc.sync.dma_start(out=bias_rows[1:2, :], in_=b_mu.rearrange("(a n) -> a n", a=1))
+        nc.sync.dma_start(out=bls[:], in_=b_ls.rearrange("(u p e) -> p u e", u=2, e=2))
+        nc.sync.dma_start(out=bmu[:], in_=b_mu.rearrange("(u p e) -> p u e", u=2, e=2))
 
-        inv_nat = keep.tile([P, H], F32)
-        minv_nat = keep.tile([P, H], F32)
-        prod_nat = keep.tile([P, H], F32)
-        inv = keep.tile([P, PACK, C], F32)
-        minv = keep.tile([P, PACK, C], F32)
-        prod = keep.tile([P, PACK, C], F32)
+        inv_nat = keep.tile([P, 2, H], F32)
+        minv_nat = keep.tile([P, 2, H], F32)
+        prod_nat = keep.tile([P, 2, H], F32)
+        inv = keep.tile([P, PACK, HALF], F32)
+        minv = keep.tile([P, PACK, HALF], F32)
+        prod = keep.tile([P, PACK, HALF], F32)
         c2_col = keep.tile([P, PACK], F32)
         grouped = {}
         codes = {}
@@ -95,62 +92,64 @@ def tile_latent_pa_s_kernel(
             for u in range(2):
                 nc.tensor.transpose(bank_cols[:, u, :], words[:, u * P : (u + 1) * P], ident[:])
 
+        def transpose_row(name, rows, r):
+            bank = psum.tile([P, 2, P], F32, tag="s1", name="row_bank")
+            word_transposes(bank[:], rows[:, r, :])
+            banks[name, r] = bank[:]
+
         def transpose_half(name, rows, g):
-            if (name, g) == ("lsc", 0):
-                bank = psum.tile([P, 2, HALF], F32, tag="s1", name="first_bank")
-            elif name == "muc":
+            if name == "muc":
                 bank = psum.tile([P, 2, HALF], F32, tag="mc", bufs=1, name="muc_bank")
             else:
                 bank = psum.tile([P, 2, HALF], F32, tag="raw", bufs=4, name="raw_bank")
             for i in range(2):
                 word_transposes(bank[:, :, i * P : (i + 1) * P], rows[:, 2 * g + i, :])
-            banks[name, g] = bank
+                banks[name, 2 * g + i] = bank[:, :, i * P : (i + 1) * P]
+            banks[name, "half", g] = bank
 
-        def transpose_row(name, rows, r):
-            bank = psum.tile([P, 2, HALF], F32, tag="raw", bufs=4, name="row_bank")
-            word_transposes(bank[:, :, (r % 2) * P : (r % 2 + 1) * P], rows[:, r, :])
-            banks[name, r // 2] = bank
+        def natural(rows, r):
+            return rows[:, r, :].rearrange("q (n e) -> q e n", e=2)
 
-        natural_lsc = lsc_rows[:, 0, :].rearrange("q (n e) -> q e n", e=2)
-        natural_muc = muc_rows[:, 0, :].rearrange("q (n e) -> q e n", e=2)
+        def ordered(tile, r):
+            return tile[:, r, :].rearrange("q (e n) -> q e n", e=2)
 
-        def ordered(tile):
-            return tile[:].rearrange("q (e n) -> q e n", e=2)
+        def natural_exp(r):
+            nc.scalar.activation(out=ordered(inv_nat, r), in_=natural(lsc_rows, r), func=ACT.Exp, scale=-1.0)
 
-        def natural_exp():
-            nc.scalar.activation(out=ordered(inv_nat), in_=natural_lsc, func=ACT.Exp, scale=-1.0)
-
-        def natural_minv():
-            nc.vector.tensor_tensor(out=ordered(minv_nat), in0=natural_muc, in1=ordered(inv_nat), op=ALU.mult)
-
-        def natural_c2():
-            nc.vector.scalar_tensor_tensor(
-                out=ordered(prod_nat),
-                in0=ordered(minv_nat),
-                scalar=1.0,
-                in1=natural_muc,
-                op0=ALU.mult,
-                op1=ALU.mult,
-                accum_out=c2_col[:, 0:1],
+        def natural_minv(r):
+            nc.vector.tensor_tensor(
+                out=ordered(minv_nat, r), in0=natural(muc_rows, r), in1=ordered(inv_nat, r), op=ALU.mult
             )
 
-        def minv_transpose():
+        def natural_c2(r):
+            nc.vector.scalar_tensor_tensor(
+                out=ordered(prod_nat, r),
+                in0=ordered(minv_nat, r),
+                scalar=1.0,
+                in1=natural(muc_rows, r),
+                op0=ALU.mult,
+                op1=ALU.mult,
+                accum_out=c2_col[:, r : r + 1],
+            )
+
+        def minv_transpose(r):
             bank = psum.tile([P, PACK, P], F32, tag="s1", name="minv_bank")
             for t in range(PACK):
                 first = HALF * (t % 2) + P * (t // 2)
-                nc.tensor.transpose(bank[:, t, :], minv_nat[:, first : first + P], ident[:])
-            banks["minv"] = bank
+                nc.tensor.transpose(bank[:, t, :], minv_nat[:, r, first : first + P], ident[:])
+            banks["minv", r] = bank
 
-        def minv_round(copy):
-            copy(out=grouped["minv"][:, 0:P, :], in_=banks["minv"][:].rearrange("p t q -> p q t"))
+        def minv_round(r):
+            nc.scalar.copy(
+                out=grouped["minv"][:, r * P : (r + 1) * P, :],
+                in_=banks["minv", r][:].rearrange("p t q -> p q t"),
+            )
 
         def values(name, r):
-            first = 2 * P * (r % 2)
-            both = banks[name, r // 2][:].bitcast(BF16)[:, :, first : first + 2 * P]
-            return both.rearrange("p u (q e) -> p u q e", e=2)
+            return banks[name, r].bitcast(BF16).rearrange("p u (q e) -> p u q e", e=2)
 
         def quarter(tile, r):
-            return tile[:, :, r * P : (r + 1) * P].rearrange("p (u e) q -> p u e q", e=2)
+            return tile[:, :, (r - 2) * P : (r - 1) * P].rearrange("p (u e) q -> p u e q", e=2)
 
         def inverse_exp(r):
             nc.scalar.activation(
@@ -182,10 +181,9 @@ def tile_latent_pa_s_kernel(
             )
 
         def cluster_round(name, tile, r):
-            cols = slice(r * P, (r + 1) * P)
             nc.gpsimd.tensor_scalar(
-                out=grouped[name][:, cols, :],
-                in0=tile[:, :, cols].rearrange("p t q -> p q t"),
+                out=grouped[name][:, r * P : (r + 1) * P, :],
+                in0=tile[:, :, (r - 2) * P : (r - 1) * P].rearrange("p t q -> p q t"),
                 scalar1=1.0,
                 scalar2=0.0,
                 op0=ALU.mult,
@@ -195,7 +193,7 @@ def tile_latent_pa_s_kernel(
         def weight_regroup(name, g):
             nc.scalar.copy(
                 out=grouped[name][:, g * HALF : (g + 1) * HALF, :].bitcast(F32),
-                in_=banks[name, g][:].rearrange("p u n -> p n u"),
+                in_=banks[name, "half", g][:].rearrange("p u n -> p n u"),
             )
 
         def first_product(name, acc):
@@ -210,25 +208,27 @@ def tile_latent_pa_s_kernel(
                     stop=True,
                 )
 
-        transpose_half("lsc", lsc_rows, 0)
-        natural_exp()
-        natural_minv()
-        natural_c2()
-        cluster_exp(1)
-        cluster_round("inv", inv, 1)
+        for r in (0, 1):
+            transpose_row("lsc", lsc_rows, r)
+        for r in (0, 1):
+            natural_exp(r)
+            natural_minv(r)
+        for r in (0, 1):
+            inverse_exp(r)
+            natural_c2(r)
         transpose_half("lsc", lsc_rows, 1)
-        transpose_row("muc", muc_rows, 1)
         transpose_half("muc", muc_rows, 1)
+        minv_transpose(0)
         cluster_exp(2)
         cluster_round("inv", inv, 2)
-        cluster_exp(3)
-        inverse_exp(0)
-        inverse_exp(3)
-        cluster_minv(1)
         cluster_minv(2)
-        cluster_round("minv", minv, 1)
         cluster_round("minv", minv, 2)
-        cluster_prod(1)
+        cluster_exp(3)
+        cluster_minv(3)
+        cluster_round("minv", minv, 3)
+        inverse_exp(3)
+        cluster_prod(2)
+        cluster_prod(3)
 
         x_bank = psum.tile([P, 2, B], F32, tag="xe", bufs=1)
         word_transposes(x_bank[:], x_rows[:])
@@ -236,10 +236,6 @@ def tile_latent_pa_s_kernel(
         nc.scalar.copy(out=x_grouped[:].bitcast(F32), in_=x_bank[:].rearrange("p u n -> p n u"))
         x_codes = keep.tile([P, B], U32, align_bytes=64)
         x_scales = keep.tile([P, B], U8, align_bytes=64)
-        minv_transpose()
-        cluster_minv(3)
-        cluster_round("minv", minv, 3)
-        cluster_prod(2)
         nc.vector.quantize_mx(
             out=x_codes[:].bitcast(FP8X4),
             scales=x_scales[:],
@@ -249,31 +245,29 @@ def tile_latent_pa_s_kernel(
             transpose_half("ls", w_rows["ls"], g)
             weight_regroup("ls", g)
             quantise_half("ls", g)
-        cluster_prod(3)
+        quantise_half("inv", 0)
         for g in range(2):
             transpose_half("mu", w_rows["mu"], g)
             weight_regroup("mu", g)
             quantise_half("mu", g)
-        minv_round(nc.scalar.copy)
-        eb_bank = psum.tile([P, 2, 2 * P], F32, tag="xe", bufs=1)
-        word_transposes(eb_bank[:, :, 0:P], eps_rows[:])
-        word_transposes(eb_bank[:, :, P : 2 * P], bias_rows[:])
+        eb_bank = psum.tile([P, 2, P], F32, tag="xe", bufs=1)
+        word_transposes(eb_bank[:], eps_rows[:])
         eb_values = eb_bank[:].bitcast(BF16)
         half_bls = keep.tile([P, 2, 2], F32)
-        bmu = keep.tile([P, 2, 2], F32)
-        nc.scalar.mul(half_bls[:], eb_values[:, :, 2 * P : 2 * P + 2], 0.5)
-        nc.scalar.copy(out=bmu[:], in_=eb_values[:, :, 2 * P + 2 : 2 * P + 4])
-        quantise_half("inv", 0)
+        nc.scalar.mul(half_bls[:], bls[:], 0.5)
+        minv_transpose(1)
+        minv_round(0)
         quantise_half("inv", 1)
+        quantise_half("minv", 1)
         def c2_transposes(r):
-            if r == PACK - 1:
-                bank = psum.tile([P, P], F32, tag="mc", bufs=1, name="part_bank")
-            else:
+            if r == 2:
                 bank = psum.tile([P, P], F32, tag="raw", bufs=4, name="part_bank")
+            else:
+                bank = psum.tile([P, P], F32, tag="mc", bufs=1, name="part_bank")
             for t in range(PACK):
                 nc.tensor.matmul(
                     out=bank[:],
-                    lhsT=prod[:, t, r * P : (r + 1) * P],
+                    lhsT=prod[:, t, (r - 2) * P : (r - 1) * P],
                     rhs=ident[:],
                     start=t == 0,
                     stop=t == PACK - 1,
@@ -283,19 +277,17 @@ def tile_latent_pa_s_kernel(
 
         def c2_sum(r):
             nc.scalar.activation(
-                out=part_scratch[:, r, :], in_=banks["part", r][:], func=ACT.Copy, accum_out=c2_col[:, r : r + 1]
+                out=part_scratch[:, r - 2, :], in_=banks["part", r][:], func=ACT.Copy, accum_out=c2_col[:, r : r + 1]
             )
 
-        part_scratch = keep.tile([P, PACK, P], F32)
+        part_scratch = keep.tile([P, 2, P], F32)
 
-        c2_transposes(1)
-        c2_sum(1)
-        ls_acc = psum.tile([P, PACK, B], F32, tag="s1", name="ls_acc")
+        ls_acc = psum.tile([P, PACK, B], F32, tag="raw", bufs=4, name="ls_acc")
         first_product("ls", ls_acc)
         mu_acc = psum.tile([P, PACK, B], F32, tag="raw", bufs=4, name="mu_acc")
         first_product("mu", mu_acc)
-        c2_transposes(2)
-        c2_transposes(3)
+        for r in (2, 3):
+            c2_transposes(r)
 
         s_sb = keep.tile([P, PACK, B], F32)
         w_sb = keep.tile([P, PACK, B], F32)
@@ -325,14 +317,14 @@ def tile_latent_pa_s_kernel(
             )
             nc.tensor.transpose(z_bank[:, t, :], z_sb[:, t, :], ident[:])
 
+        minv_round(1)
         scaled_noise(0)
         scaled_noise(1)
-        latent(0)
-        scaled_noise(2)
-        latent(1)
-        scaled_noise(3)
-        latent(2)
-        latent(3)
+        for t in range(2, PACK):
+            latent(t - 2)
+            scaled_noise(t)
+        latent(PACK - 2)
+        latent(PACK - 1)
         for r in (2, 3):
             c2_sum(r)
         quantise_half("minv", 0)
@@ -341,7 +333,6 @@ def tile_latent_pa_s_kernel(
         z_view = z_sb[:].rearrange("p t b -> p b t")
         nc.vector.tensor_scalar_mul(out=z_grouped[:, 0, :, :], in0=z_view, scalar1=-2.0)
         nc.scalar.activation(out=z_grouped[:, 1, :, :], in_=z_view, func=ACT.Square)
-        quantise_half("minv", 1)
         z_codes = keep.tile([P, 2 * B], U32, align_bytes=64)
         z_scales = keep.tile([P, 2 * B], U8, align_bytes=64)
         for a in range(2):
@@ -397,9 +388,8 @@ def tile_latent_pa_s_kernel(
         )
         e_rec = keep.tile([P, 1], F32)
         nc.vector.reciprocal(out=e_rec[:], in_=e_sum[:])
-        att = keep.tile([P, P, PACK], F32)
-        e_view = e_sb[:].rearrange("b (r q) -> b q r", r=PACK)
-        nc.vector.tensor_scalar_mul(out=att[:, 0:64, :], in0=e_view[:, 0:64, :], scalar1=e_rec[:])
-        nc.scalar.activation(out=att[:, 64:P, :], in_=e_view[:, 64:P, :], func=ACT.Copy, scale=e_rec[:])
-        nc.sync.dma_start(out=out_1[:, 0:HALF], in_=att[:, 0:64, :].rearrange("b q r -> b (q r)"))
-        nc.scalar.dma_start(out=out_1[:, HALF:C], in_=att[:, 64:P, :].rearrange("b q r -> b (q r)"))
+        att = keep.tile([P, C], F32)
+        nc.vector.tensor_scalar_mul(out=att[:, 0:HALF], in0=e_sb[:, 0:HALF], scalar1=e_rec[:])
+        nc.scalar.activation(out=att[:, HALF:C], in_=e_sb[:, HALF:C], func=ACT.Copy, scale=e_rec[:])
+        nc.sync.dma_start(out=out_1[:, 0:HALF], in_=att[:, 0:HALF])
+        nc.scalar.dma_start(out=out_1[:, HALF:C], in_=att[:, HALF:C])

@@ -289,6 +289,16 @@ def tile_latent_pa_s_kernel(
         for r in (2, 3):
             c2_transposes(r)
 
+        c2_bank = psum.tile([P, C], F32, tag="s1")
+        for r in (0, 1):
+            nc.tensor.matmul(
+                out=c2_bank[:, r * P : (r + 1) * P],
+                lhsT=c2_col[:, r : r + 1].to_broadcast([P, P]),
+                rhs=ident[:],
+                start=True,
+                stop=True,
+            )
+
         s_sb = keep.tile([P, PACK, B], F32)
         w_sb = keep.tile([P, PACK, B], F32)
         z_sb = keep.tile([P, PACK, B], F32)
@@ -341,8 +351,7 @@ def tile_latent_pa_s_kernel(
                 scales=z_scales[:, a * B : (a + 1) * B],
                 in_=z_grouped[:, a, :, :].rearrange("p b t -> p (b t)"),
             )
-        c2_bank = psum.tile([P, C], F32, tag="s1")
-        for r in range(PACK):
+        for r in (2, 3):
             nc.tensor.transpose(
                 c2_bank[:, r * P : (r + 1) * P], c2_col[:, r : r + 1].to_broadcast([P, P]), ident[:]
             )

from contextlib import ExitStack

import concourse.mybir as mybir
from concourse.masks import make_identity

F32 = mybir.dt.float32
BF16 = mybir.dt.bfloat16
U32 = mybir.dt.uint32
U8 = mybir.dt.uint8
FP8X4 = mybir.dt.float8_e4m3fn_x4
ACT = mybir.ActivationFunctionType
ALU = mybir.AluOpType
AX = mybir.AxisListType

P = 128
PACK = 4
B = 128
H = 512
C = 512
HALF = 256

FLOPS = 4 * 2 * B * H * 512


def tile_latent_pa_s_kernel(
    tc, encoder_final_state, W_mu, b_mu, W_ls, b_ls, mu_c, log_sigma_sq_c, eps_z, out_0, out_1
):
    nc = tc.nc
    with ExitStack() as ctx:
        keep = ctx.enter_context(tc.tile_pool(name="keep", bufs=1))
        psum = ctx.enter_context(tc.psum_pool(name="psum", bufs=2))
        ctx.enter_context(tc.manual_schedule())

        ident = keep.tile([P, P], F32)
        make_identity(nc, ident[:])

        bls = keep.tile([P, 2, 2], BF16)
        bmu = keep.tile([P, 2, 2], BF16)
        lsc_rows = keep.tile([P, PACK, H], BF16)
        muc_rows = keep.tile([P, PACK, H], BF16)
        lsc_dram = log_sigma_sq_c.rearrange("(r q) h -> q r h", r=PACK)
        muc_dram = mu_c.rearrange("(r q) h -> q r h", r=PACK)
        x_rows = keep.tile([P, H], BF16)
        w_rows = {}
        for name in ("ls", "mu"):
            w_rows[name] = keep.tile([P, PACK, H], BF16, name="w_rows_" + name)
        eps_rows = keep.tile([P, H], BF16)

        def load_rows(rows, dram, first, last):
            nc.sync.dma_start(out=rows[:, first:last, :], in_=dram[:, first:last, :])

        def load_weight(name, dram):
            view = dram.rearrange("(u q e) k -> q u e k", u=2, e=2)
            nc.sync.dma_start(out=w_rows[name][:].rearrange("q (u e) k -> q u e k", e=2), in_=view)

        for first, last in ((0, 1), (1, 2), (2, PACK)):
            load_rows(lsc_rows, lsc_dram, first, last)
            load_rows(muc_rows, muc_dram, first, last)
        nc.sync.dma_start(out=x_rows[:], in_=encoder_final_state)
        load_weight("ls", W_ls)
        load_weight("mu", W_mu)
        nc.sync.dma_start(out=eps_rows[:], in_=eps_z)
        nc.sync.dma_start(out=bls[:], in_=b_ls.rearrange("(u p e) -> p u e", u=2, e=2))
        nc.sync.dma_start(out=bmu[:], in_=b_mu.rearrange("(u p e) -> p u e", u=2, e=2))

        inv_nat = keep.tile([P, 2, H], F32)
        minv_nat = keep.tile([P, 2, H], F32)
        prod_nat = keep.tile([P, 2, H], F32)
        inv = keep.tile([P, PACK, HALF], F32)
        minv = keep.tile([P, PACK, HALF], F32)
        prod = keep.tile([P, PACK, HALF], F32)
        c2_col = keep.tile([P, PACK], F32)
        grouped = {}
        codes = {}
        scales = {}
        for name in ("inv", "minv", "ls", "mu"):
            grouped[name] = keep.tile([P, C, PACK], BF16, align_bytes=64, name="grouped_" + name)
            codes[name] = keep.tile([P, C], U32, align_bytes=64, name="codes_" + name)
            scales[name] = keep.tile([P, C], U8, align_bytes=64, name="scales_" + name)
        banks = {}

        def quantise_half(name, g):
            cols = slice(g * HALF, (g + 1) * HALF)
            nc.vector.quantize_mx(
                out=codes[name][:, cols].bitcast(FP8X4),
                scales=scales[name][:, cols],
                in_=grouped[name][:, cols, :].rearrange("p n t -> p (n t)"),
            )

        def word_transposes(bank_cols, rows):
            words = rows.bitcast(F32)
            for u in range(2):
                nc.tensor.transpose(bank_cols[:, u, :], words[:, u * P : (u + 1) * P], ident[:])

        def transpose_row(name, rows, r):
            bank = psum.tile([P, 2, P], F32, tag="s1", name="row_bank")
            word_transposes(bank[:], rows[:, r, :])
            banks[name, r] = bank[:]

        def transpose_half(name, rows, g):
            if name == "muc":
                bank = psum.tile([P, 2, HALF], F32, tag="mc", bufs=1, name="muc_bank")
            else:
                bank = psum.tile([P, 2, HALF], F32, tag="raw", bufs=4, name="raw_bank")
            for i in range(2):
                word_transposes(bank[:, :, i * P : (i + 1) * P], rows[:, 2 * g + i, :])
                banks[name, 2 * g + i] = bank[:, :, i * P : (i + 1) * P]
            banks[name, "half", g] = bank

        def natural(rows, r):
            return rows[:, r, :].rearrange("q (n e) -> q e n", e=2)

        def ordered(tile, r):
            return tile[:, r, :].rearrange("q (e n) -> q e n", e=2)

        def natural_exp(r):
            nc.scalar.activation(out=ordered(inv_nat, r), in_=natural(lsc_rows, r), func=ACT.Exp, scale=-1.0)

        def natural_minv(r):
            nc.vector.tensor_tensor(
                out=ordered(minv_nat, r), in0=natural(muc_rows, r), in1=ordered(inv_nat, r), op=ALU.mult
            )

        def natural_c2(r):
            nc.vector.scalar_tensor_tensor(
                out=ordered(prod_nat, r),
                in0=ordered(minv_nat, r),
                scalar=1.0,
                in1=natural(muc_rows, r),
                op0=ALU.mult,
                op1=ALU.mult,
                accum_out=c2_col[:, r : r + 1],
            )

        def minv_transpose(r):
            bank = psum.tile([P, PACK, P], F32, tag="s1", name="minv_bank")
            for t in range(PACK):
                first = HALF * (t % 2) + P * (t // 2)
                nc.tensor.transpose(bank[:, t, :], minv_nat[:, r, first : first + P], ident[:])
            banks["minv", r] = bank

        def minv_round(r):
            nc.scalar.copy(
                out=grouped["minv"][:, r * P : (r + 1) * P, :],
                in_=banks["minv", r][:].rearrange("p t q -> p q t"),
            )

        def values(name, r):
            return banks[name, r].bitcast(BF16).rearrange("p u (q e) -> p u q e", e=2)

        def quarter(tile, r):
            return tile[:, :, (r - 2) * P : (r - 1) * P].rearrange("p (u e) q -> p u e q", e=2)

        def inverse_exp(r):
            nc.scalar.activation(
                out=grouped["inv"][:, r * P : (r + 1) * P, :].rearrange("p q (u e) -> p q u e", e=2),
                in_=values("lsc", r).rearrange("p u q e -> p q u e"),
                func=ACT.Exp,
                scale=-1.0,
            )

        def cluster_exp(r):
            nc.scalar.activation(
                out=quarter(inv, r), in_=values("lsc", r).rearrange("p u q e -> p u e q"), func=ACT.Exp, scale=-1.0
            )

        def cluster_minv(r):
            nc.vector.tensor_tensor(
                out=quarter(minv, r),
                in0=values("muc", r).rearrange("p u q e -> p u e q"),
                in1=quarter(inv, r),
                op=ALU.mult,
            )

        def cluster_prod(r):
            nc.vector.tensor_tensor(
                out=quarter(prod, r),
                in0=values("muc", r).rearrange("p u q e -> p u e q"),
                in1=quarter(minv, r),
                op=ALU.mult,
            )

        def cluster_round(name, tile, r):
            nc.gpsimd.tensor_scalar(
                out=grouped[name][:, r * P : (r + 1) * P, :],
                in0=tile[:, :, (r - 2) * P : (r - 1) * P].rearrange("p t q -> p q t"),
                scalar1=1.0,
                scalar2=0.0,
                op0=ALU.mult,
                op1=ALU.add,
            )

        def weight_regroup(name, g):
            nc.scalar.copy(
                out=grouped[name][:, g * HALF : (g + 1) * HALF, :].bitcast(F32),
                in_=banks[name, "half", g][:].rearrange("p u n -> p n u"),
            )

        def first_product(name, acc):
            for t in range(PACK):
                nc.tensor.matmul_mx(
                    out=acc[:, t, :],
                    lhsT=codes[name][:, t * P : (t + 1) * P].bitcast(FP8X4),
                    lhsT_scale=scales[name][:, t * P : (t + 1) * P],
                    rhs=x_codes[:].bitcast(FP8X4),
                    rhs_scale=x_scales[:],
                    start=True,
                    stop=True,
                )

        for r in (0, 1):
            transpose_row("lsc", lsc_rows, r)
        for r in (0, 1):
            natural_exp(r)
            natural_minv(r)
        for r in (0, 1):
            inverse_exp(r)
            natural_c2(r)
        transpose_half("lsc", lsc_rows, 1)
        transpose_half("muc", muc_rows, 1)
        minv_transpose(0)
        cluster_exp(2)
        cluster_round("inv", inv, 2)
        cluster_minv(2)
        cluster_round("minv", minv, 2)
        cluster_exp(3)
        cluster_minv(3)
        cluster_round("minv", minv, 3)
        inverse_exp(3)
        cluster_prod(2)
        cluster_prod(3)

        x_bank = psum.tile([P, 2, B], F32, tag="xe", bufs=1)
        word_transposes(x_bank[:], x_rows[:])
        x_grouped = keep.tile([P, B, PACK], BF16, align_bytes=64)
        nc.scalar.copy(out=x_grouped[:].bitcast(F32), in_=x_bank[:].rearrange("p u n -> p n u"))
        x_codes = keep.tile([P, B], U32, align_bytes=64)
        x_scales = keep.tile([P, B], U8, align_bytes=64)
        nc.vector.quantize_mx(
            out=x_codes[:].bitcast(FP8X4),
            scales=x_scales[:],
            in_=x_grouped[:].rearrange("p n t -> p (n t)"),
        )
        for g in range(2):
            transpose_half("ls", w_rows["ls"], g)
            weight_regroup("ls", g)
            quantise_half("ls", g)
        quantise_half("inv", 0)
        for g in range(2):
            transpose_half("mu", w_rows["mu"], g)
            weight_regroup("mu", g)
            quantise_half("mu", g)
        eb_bank = psum.tile([P, 2, P], F32, tag="xe", bufs=1)
        word_transposes(eb_bank[:], eps_rows[:])
        eb_values = eb_bank[:].bitcast(BF16)
        half_bls = keep.tile([P, 2, 2], F32)
        nc.scalar.mul(half_bls[:], bls[:], 0.5)
        minv_transpose(1)
        minv_round(0)
        quantise_half("inv", 1)
        quantise_half("minv", 1)
        def c2_transposes(r):
            if r == 2:
                bank = psum.tile([P, P], F32, tag="raw", bufs=4, name="part_bank")
            else:
                bank = psum.tile([P, P], F32, tag="mc", bufs=1, name="part_bank")
            for t in range(PACK):
                nc.tensor.matmul(
                    out=bank[:],
                    lhsT=prod[:, t, (r - 2) * P : (r - 1) * P],
                    rhs=ident[:],
                    start=t == 0,
                    stop=t == PACK - 1,
                    is_transpose=True,
                )
            banks["part", r] = bank

        def c2_sum(r):
            nc.scalar.activation(
                out=part_scratch[:, r - 2, :], in_=banks["part", r][:], func=ACT.Copy, accum_out=c2_col[:, r : r + 1]
            )

        part_scratch = keep.tile([P, 2, P], F32)

        ls_acc = psum.tile([P, PACK, B], F32, tag="raw", bufs=4, name="ls_acc")
        first_product("ls", ls_acc)
        mu_acc = psum.tile([P, PACK, B], F32, tag="raw", bufs=4, name="mu_acc")
        first_product("mu", mu_acc)
        for r in (2, 3):
            c2_transposes(r)

        c2_bank = psum.tile([P, C], F32, tag="s1")
        for r in (0, 1):
            nc.tensor.matmul(
                out=c2_bank[:, r * P : (r + 1) * P],
                lhsT=c2_col[:, r : r + 1].to_broadcast([P, P]),
                rhs=ident[:],
                start=True,
                stop=True,
            )

        s_sb = keep.tile([P, PACK, B], F32)
        w_sb = keep.tile([P, PACK, B], F32)
        z_sb = keep.tile([P, PACK, B], F32)
        z_bank = psum.tile([P, PACK, P], F32, tag="raw", bufs=4)
        for t in range(PACK):
            nc.scalar.activation(
                out=s_sb[:, t, :],
                in_=ls_acc[:, t, :],
                func=ACT.Exp,
                bias=half_bls[:, t // 2, t % 2 : t % 2 + 1],
                scale=0.5,
            )

        def scaled_noise(t):
            eps_t = eb_values[:, t // 2, 0 : 2 * P].rearrange("p (b e) -> p e b", e=2)[:, t % 2, :]
            nc.vector.tensor_tensor(out=w_sb[:, t, :], in0=s_sb[:, t, :], in1=eps_t, op=ALU.mult)

        def latent(t):
            nc.vector.scalar_tensor_tensor(
                out=z_sb[:, t, :],
                in0=mu_acc[:, t, :],
                scalar=bmu[:, t // 2, t % 2 : t % 2 + 1],
                in1=w_sb[:, t, :],
                op0=ALU.add,
                op1=ALU.add,
            )
            nc.tensor.transpose(z_bank[:, t, :], z_sb[:, t, :], ident[:])

        minv_round(1)
        scaled_noise(0)
        scaled_noise(1)
        for t in range(2, PACK):
            latent(t - 2)
            scaled_noise(t)
        latent(PACK - 2)
        latent(PACK - 1)
        for r in (2, 3):
            c2_sum(r)
        quantise_half("minv", 0)

        z_grouped = keep.tile([P, 2, B, PACK], BF16, align_bytes=64)
        z_view = z_sb[:].rearrange("p t b -> p b t")
        nc.vector.tensor_scalar_mul(out=z_grouped[:, 0, :, :], in0=z_view, scalar1=-2.0)
        nc.scalar.activation(out=z_grouped[:, 1, :, :], in_=z_view, func=ACT.Square)
        z_codes = keep.tile([P, 2 * B], U32, align_bytes=64)
        z_scales = keep.tile([P, 2 * B], U8, align_bytes=64)
        for a in range(2):
            nc.vector.quantize_mx(
                out=z_codes[:, a * B : (a + 1) * B].bitcast(FP8X4),
                scales=z_scales[:, a * B : (a + 1) * B],
                in_=z_grouped[:, a, :, :].rearrange("p b t -> p (b t)"),
            )
        for r in (2, 3):
            nc.tensor.transpose(
                c2_bank[:, r * P : (r + 1) * P], c2_col[:, r : r + 1].to_broadcast([P, P]), ident[:]
            )
        c2_sb = keep.tile([P, C], F32)
        nc.scalar.copy(out=c2_sb[:], in_=c2_bank[:])

        z_out = keep.tile([P, H], F32)
        nc.scalar.copy(
            out=z_out[:].rearrange("b (u p e) -> b u p e", u=2, e=2),
            in_=z_bank[:].rearrange("b (u e) p -> b u p e", e=2),
        )
        nc.sync.dma_start(out=out_0, in_=z_out[:])

        d_banks = [psum.tile([P, HALF], F32, tag="raw", bufs=4, name="d_bank") for g in range(2)]

        def second_product(a, name, start, g):
            cols = slice(g * HALF, (g + 1) * HALF)
            nc.tensor.matmul_mx(
                out=d_banks[g][:],
                lhsT=z_codes[:, a * B : (a + 1) * B].bitcast(FP8X4),
                lhsT_scale=z_scales[:, a * B : (a + 1) * B],
                rhs=codes[name][:, cols].bitcast(FP8X4),
                rhs_scale=scales[name][:, cols],
                start=start,
                stop=not start,
            )

        for g in range(2):
            second_product(0, "minv", True, g)
        for g in range(2):
            second_product(1, "inv", False, g)

        d_sb = keep.tile([P, C], F32)
        for g in range(2):
            cols = slice(g * HALF, (g + 1) * HALF)
            nc.vector.tensor_tensor(out=d_sb[:, cols], in0=d_banks[g][:], in1=c2_sb[:, cols], op=ALU.add)
        d_min = keep.tile([P, 1], F32)
        nc.vector.tensor_reduce(out=d_min[:], in_=d_sb[:], axis=AX.X, op=ALU.min)
        e_sb = keep.tile([P, C], F32)
        e_sum = keep.tile([P, 1], F32)
        nc.scalar.activation(
            out=e_sb[:], in_=d_sb[:], func=ACT.Exp, bias=d_min[:], scale=-1.0, accum_out=e_sum[:]
        )
        e_rec = keep.tile([P, 1], F32)
        nc.vector.reciprocal(out=e_rec[:], in_=e_sum[:])
        att = keep.tile([P, C], F32)
        nc.vector.tensor_scalar_mul(out=att[:, 0:HALF], in0=e_sb[:, 0:HALF], scalar1=e_rec[:])
        nc.scalar.activation(out=att[:, HALF:C], in_=e_sb[:, HALF:C], func=ACT.Copy, scale=e_rec[:])
        nc.sync.dma_start(out=out_1[:, 0:HALF], in_=att[:, 0:HALF])
        nc.scalar.dma_start(out=out_1[:, HALF:C], in_=att[:, HALF:C])
